import numpy as np
import ml_dtypes


def mxq(x, axis, fmt="e4m3"):
    dtype, down = {"e4m3": (ml_dtypes.float8_e4m3fn, 7), "e5m2": (ml_dtypes.float8_e5m2, 14)}[fmt]
    v = np.moveaxis(np.asarray(x, np.float32).astype(ml_dtypes.bfloat16).astype(np.float64), axis, -1)
    blocks = v.reshape(v.shape[:-1] + (-1, 32))
    amax = np.abs(blocks).max(-1, keepdims=True)
    byte = np.maximum(np.where(amax > 0, np.frexp(amax)[1] - 1 + 127, 0) - down, 1)
    scale = np.exp2(byte - 127.0)
    codes = (blocks / scale).astype(np.float32).astype(dtype).astype(np.float64)
    return np.moveaxis((codes * scale).reshape(v.shape), -1, axis)


WIDE = False


def mx_kscale(k):
    if not WIDE:
        return np.ones(k)
    levels = np.array([10, -10, 5, -5, 0])
    a = np.random.permutation(np.resize(levels, k // 512 * 4)).reshape(k // 512, 4)
    idx = np.arange(k)
    return np.exp2(a[idx // 512, idx % 128 // 32])


BF16 = ml_dtypes.bfloat16


def bf(x):
    return np.asarray(x, np.float32).astype(BF16)


def f64(x):
    return np.asarray(x).astype(np.float64)


NB, C, O, CZ, DD, HH, WW, MG = 1, 8192, 512, 512, 2, 4, 16, 4
STRIDES = (2, 2, 2)


def setup_inputs():
    s = mx_kscale(C)
    sd, sh, sw = STRIDES
    return {"x": bf(np.random.standard_normal((NB, C, DD, HH, WW)) * s[None, :, None, None, None]),
            "z": bf(np.random.standard_normal((NB, CZ, sd * DD + MG, sh * HH + MG, sw * WW + MG))),
            "W": bf(np.random.standard_normal((O, C)) / np.sqrt(C) / s[None, :]),
            "b": bf(np.random.standard_normal(O) * 0.5)}


def reference(x, z, W, b):
    sd, sh, sw = STRIDES
    u = np.repeat(np.repeat(np.repeat(f64(x), sd, axis=2), sh, axis=3), sw, axis=4)
    n, c, d, h, w = u.shape
    y = mxq(f64(W), 1, "e4m3") @ mxq(u.reshape(n, c, d * h * w), 1, "e4m3")
    y = y.reshape(n, -1, d, h, w) + f64(b)[None, :, None, None, None]
    zf = f64(z)
    off = [(zf.shape[i] - y.shape[i]) // 2 for i in range(2, 5)]
    zc = zf[:, :,
            off[0]:off[0] + y.shape[2],
            off[1]:off[1] + y.shape[3],
            off[2]:off[2] + y.shape[4]]
    return np.concatenate([y, zc], axis=1)

@@ -1,0 +1,236 @@
+from contextlib import ExitStack
+
+import concourse.mybir as mybir
+from concourse.masks import make_identity
+
+F32 = mybir.dt.float32
+BF16 = mybir.dt.bfloat16
+U32 = mybir.dt.uint32
+U8 = mybir.dt.uint8
+FP8X4 = mybir.dt.float8_e4m3fn_x4
+IDENTITY = mybir.ActivationFunctionType.Identity
+
+P = 128
+PACK = 4
+K_PASS = P * PACK
+PAIR = 2
+BANK_WORDS = 512
+
+CHANNELS = 8192
+OUT_CHANNELS = 512
+Z_CHANNELS = 512
+DEPTH = 2
+HEIGHT = 4
+WIDTH = 16
+POSITIONS = DEPTH * HEIGHT * WIDTH
+UP = 2
+UP_POSITIONS = UP * UP * UP * POSITIONS
+MARGIN = 2
+Z_HEIGHT = UP * HEIGHT + 2 * MARGIN
+Z_WIDTH = UP * WIDTH + 2 * MARGIN
+
+PASSES = CHANNELS // K_PASS
+O_TILES = OUT_CHANNELS // P
+Z_TILES = Z_CHANNELS // P
+CHUNK_PASSES = 4
+CHUNK_K = CHUNK_PASSES * K_PASS
+CHUNKS = PASSES // CHUNK_PASSES
+CHUNK_BANKS = CHUNK_K // PAIR // BANK_WORDS
+BANK_PASSES = CHUNK_PASSES // CHUNK_BANKS
+N_MOVING = UP * POSITIONS
+GROUPS = UP * UP
+TRANSPOSE_BANKS = 8 - GROUPS
+Z_O_TILE = 2
+
+FLOPS = 2 * OUT_CHANNELS * CHANNELS * UP_POSITIONS
+BYTES = (
+    2 * (CHANNELS * POSITIONS + OUT_CHANNELS * CHANNELS + OUT_CHANNELS + Z_CHANNELS * UP_POSITIONS)
+    + 4 * (OUT_CHANNELS + Z_CHANNELS) * UP_POSITIONS
+)
+
+
+def tile_upconvcropcat_k_kernel(tc, x, z, W, b, out):
+    nc = tc.nc
+    x_rows = x.rearrange("n c d h w -> (n c) (d h w)")
+    z_rows = z.rearrange("n c d h w -> (n c) d (h w)")
+    out_rows = out.rearrange("n c d h w -> (n c) (d h w)")
+
+    with ExitStack() as stack:
+        const = stack.enter_context(tc.tile_pool(name="const", bufs=1))
+        x_raw_pool = stack.enter_context(tc.tile_pool(name="x_raw", bufs=CHUNKS))
+        w_raw_pool = stack.enter_context(tc.tile_pool(name="w_raw", bufs=O_TILES * CHUNKS))
+        z_raw_pool = stack.enter_context(tc.tile_pool(name="z_raw", bufs=Z_TILES))
+        x_mx_pool = stack.enter_context(tc.tile_pool(name="x_mx", bufs=CHUNKS))
+        stage = stack.enter_context(tc.tile_pool(name="stage", bufs=3))
+        results = stack.enter_context(tc.tile_pool(name="results", bufs=2))
+        acc_pool = stack.enter_context(tc.psum_pool(name="acc", bufs=GROUPS))
+        turned_pool = stack.enter_context(tc.psum_pool(name="turned", bufs=TRANSPOSE_BANKS))
+        stack.enter_context(tc.manual_schedule())
+
+        def load_w(q):
+            m, n = divmod(q, CHUNKS)
+            w_raw = w_raw_pool.tile([P, CHUNK_K], BF16)
+            nc.sync.dma_start(out=w_raw[:], in_=W[m * P : (m + 1) * P, n * CHUNK_K : (n + 1) * CHUNK_K])
+            return w_raw
+
+        def load_x(n):
+            x_raw = x_raw_pool.tile([P, CHUNK_K], BF16)
+            nc.sync.dma_start(
+                out=x_raw[:].rearrange("p (s f) -> p s f", f=PAIR * POSITIONS),
+                in_=x_rows[n * CHUNK_K : (n + 1) * CHUNK_K, :].rearrange("(s q e) w -> q s (e w)", q=P, e=PAIR),
+            )
+            return x_raw
+
+        def load_z(i):
+            z_raw = z_raw_pool.tile([P, UP * DEPTH * Z_HEIGHT * Z_WIDTH], BF16)
+            nc.sync.dma_start(
+                out=z_raw[:],
+                in_=z_rows[i * P : (i + 1) * P, MARGIN : MARGIN + UP * DEPTH, :].rearrange("c d f -> c (d f)"),
+            )
+            return z_raw
+
+        x_raws = []
+        w_raws = []
+        z_raws = []
+        for n in range(CHUNKS):
+            x_raws.append(load_x(n))
+            w_raws.append(load_w(n))
+        for q in range(CHUNKS, (O_TILES - 1) * CHUNKS):
+            w_raws.append(load_w(q))
+        for i in range(Z_TILES):
+            z_raws.append(load_z(i))
+        for q in range((O_TILES - 1) * CHUNKS, O_TILES * CHUNKS):
+            w_raws.append(load_w(q))
+
+        identity = const.tile([P, P], F32)
+        make_identity(nc, identity[:])
+
+        b_rows = const.tile([P, P], BF16)
+        nc.vector.memset(b_rows[:], 0.0)
+        nc.scalar.dma_start(out=b_rows[0:O_TILES, :], in_=b.rearrange("(m o) -> m o", m=O_TILES))
+        b_rows_f32 = const.tile([P, P], F32)
+        nc.vector.tensor_copy(out=b_rows_f32[:], in_=b_rows[:])
+        b_turned = turned_pool.tile([P, BANK_WORDS], F32, tag="turned")
+        nc.tensor.transpose(out=b_turned[:, 0:P], in_=b_rows_f32[:], identity=identity[:])
+        bias = const.tile([P, O_TILES], F32)
+        nc.scalar.activation(out=bias[:], in_=b_turned[:, 0:O_TILES], func=IDENTITY)
+
+        x_words = []
+        x_scales = []
+
+        def regroup_x(n):
+            x_grouped = stage.tile([P, CHUNK_K], BF16, align_bytes=64)
+            for g in range(CHUNK_PASSES):
+                cols = slice(g * K_PASS, (g + 1) * K_PASS)
+                copy = nc.vector.tensor_copy if g % 2 == 0 else nc.scalar.copy
+                copy(
+                    out=x_grouped[:, cols].rearrange("p (c i t) -> p c t i", i=4, t=PACK),
+                    in_=x_raws[n][:, cols].rearrange("p (t c i) -> p c t i", t=PACK, i=4),
+                )
+            return x_grouped
+
+        def quantise_x(x_grouped):
+            words = x_mx_pool.tile([P, CHUNK_PASSES * N_MOVING], U32, align_bytes=64)
+            scales = x_mx_pool.tile([P, CHUNK_PASSES * N_MOVING], U8, align_bytes=64)
+            for g in range(CHUNK_PASSES):
+                for r in range(UP):
+                    cols = slice(g * N_MOVING + r * POSITIONS, g * N_MOVING + (r + 1) * POSITIONS)
+                    nc.vector.quantize_mx(
+                        out=words[:, cols].bitcast(FP8X4),
+                        scales=scales[:, cols],
+                        in_=x_grouped[:, g * K_PASS : (g + 1) * K_PASS],
+                    )
+            x_words.append(words)
+            x_scales.append(scales)
+
+        def transpose_w(q):
+            raw_words = w_raws[q][:].bitcast(F32)
+            w_grouped = stage.tile([P, CHUNK_K], BF16, align_bytes=64)
+            grouped_words = w_grouped[:].bitcast(F32)
+            for h in range(CHUNK_BANKS):
+                turned = turned_pool.tile([P, BANK_WORDS], F32, tag="turned")
+                for s in range(BANK_WORDS // P):
+                    nc.tensor.transpose(
+                        out=turned[:, s * P : (s + 1) * P],
+                        in_=raw_words[:, h * BANK_WORDS + s * P : h * BANK_WORDS + (s + 1) * P],
+                        identity=identity[:],
+                    )
+                nc.scalar.copy(
+                    out=grouped_words[:, h * BANK_WORDS : (h + 1) * BANK_WORDS].rearrange(
+                        "p (g o u) -> p g o u", g=BANK_PASSES, u=PAIR
+                    ),
+                    in_=turned[:].rearrange("p (g u o) -> p g o u", g=BANK_PASSES, u=PAIR),
+                )
+            return w_grouped
+
+        def quantise_w(w_grouped):
+            words = stage.tile([P, CHUNK_PASSES * P], U32, align_bytes=64)
+            scales = stage.tile([P, CHUNK_PASSES * P], U8, align_bytes=64)
+            nc.vector.quantize_mx(out=words[:].bitcast(FP8X4), scales=scales[:], in_=w_grouped[:])
+            return words, scales
+
+        def prepare(q):
+            if q < CHUNKS:
+                x_grouped = regroup_x(q)
+            w_grouped = transpose_w(q)
+            if q < CHUNKS:
+                quantise_x(x_grouped)
+            return quantise_w(w_grouped)
+
+        def multiply(n, w_words, w_scales, acc):
+            for g in range(CHUNK_PASSES):
+                c = n * CHUNK_PASSES + g
+                o_cols = slice(g * P, (g + 1) * P)
+                x_cols = slice(g * N_MOVING, (g + 1) * N_MOVING)
+                for group in acc:
+                    nc.tensor.matmul_mx(
+                        out=group[:],
+                        lhsT=w_words[:, o_cols].bitcast(FP8X4),
+                        lhsT_scale=w_scales[:, o_cols],
+                        rhs=x_words[n][:, x_cols].bitcast(FP8X4),
+                        rhs_scale=x_scales[n][:, x_cols],
+                        start=(c == 0),
+                        stop=(c == PASSES - 1),
+                    )
+
+        def finish(m, acc):
+            y = results.tile([P, UP_POSITIONS], F32)
+            y_view = y[:].rearrange(
+                "p (i a h b k r) -> p a b i h k r", i=DEPTH, a=UP, h=HEIGHT, b=UP, k=WIDTH, r=UP
+            )
+            for j in range(GROUPS):
+                y_part = y_view[:, j // UP, j % UP]
+                sums = acc[j][:].rearrange("p (r i h k) -> p i h k r", r=UP, i=DEPTH, h=HEIGHT)
+                if j % 2 == 0:
+                    nc.scalar.activation(out=y_part, in_=sums, func=IDENTITY, bias=bias[:, m : m + 1])
+                else:
+                    nc.vector.tensor_scalar_add(out=y_part, in0=sums, scalar1=bias[:, m : m + 1])
+            nc.sync.dma_start(out=out_rows[m * P : (m + 1) * P, :], in_=y[:])
+
+        def crop_z(i):
+            cropped = results.tile([P, UP_POSITIONS], F32)
+            nc.vector.tensor_copy(
+                out=cropped[:].rearrange("p (d h w) -> p d h w", h=UP * HEIGHT, w=UP * WIDTH),
+                in_=z_raws[i][:].rearrange("p (d h w) -> p d h w", h=Z_HEIGHT, w=Z_WIDTH)[
+                    :, :, MARGIN : MARGIN + UP * HEIGHT, MARGIN : MARGIN + UP * WIDTH
+                ],
+            )
+            nc.sync.dma_start(out=out_rows[OUT_CHANNELS + i * P : OUT_CHANNELS + (i + 1) * P, :], in_=cropped[:])
+
+        ready = prepare(0)
+        acc = []
+        for q in range(O_TILES * CHUNKS):
+            m, n = divmod(q, CHUNKS)
+            w_words, w_scales = ready
+            if q + 1 < O_TILES * CHUNKS:
+                ready = prepare(q + 1)
+            if n == 0:
+                acc = []
+                for j in range(GROUPS):
+                    group = acc_pool.tile([P, N_MOVING], F32)
+                    acc.append(group)
+            multiply(n, w_words, w_scales, acc)
+            if m == Z_O_TILE:
+                crop_z(n)
+            if n == CHUNKS - 1:
+                finish(m, acc)

@@ -15,6 +15,7 @@ PACK = 4
 K_PASS = P * PACK
 PAIR = 2
 BANK_WORDS = 512
+PSUM_BANKS = 8
 
 CHANNELS = 8192
 OUT_CHANNELS = 512
@@ -24,7 +25,8 @@ HEIGHT = 4
 WIDTH = 16
 POSITIONS = DEPTH * HEIGHT * WIDTH
 UP = 2
-UP_POSITIONS = UP * UP * UP * POSITIONS
+UP_PLANE = UP * HEIGHT * UP * WIDTH
+UP_POSITIONS = UP * DEPTH * UP_PLANE
 MARGIN = 2
 Z_HEIGHT = UP * HEIGHT + 2 * MARGIN
 Z_WIDTH = UP * WIDTH + 2 * MARGIN
@@ -32,14 +34,17 @@ Z_WIDTH = UP * WIDTH + 2 * MARGIN
 PASSES = CHANNELS // K_PASS
 O_TILES = OUT_CHANNELS // P
 Z_TILES = Z_CHANNELS // P
-CHUNK_PASSES = 4
-CHUNK_K = CHUNK_PASSES * K_PASS
-CHUNKS = PASSES // CHUNK_PASSES
-CHUNK_BANKS = CHUNK_K // PAIR // BANK_WORDS
-BANK_PASSES = CHUNK_PASSES // CHUNK_BANKS
 N_MOVING = UP * POSITIONS
 GROUPS = UP * UP
-TRANSPOSE_BANKS = 8 - GROUPS
+
+PIECE_PASSES = 4
+PIECE_K = PIECE_PASSES * K_PASS
+PIECES = PASSES // PIECE_PASSES
+PIECE_BANKS = PIECE_K // PAIR // BANK_WORDS
+BANK_PASSES = PIECE_PASSES // PIECE_BANKS
+RUN_PIECES = (PSUM_BANKS - GROUPS) // PIECE_BANKS
+CHUNKS = PIECES // RUN_PIECES
+ALL_CHUNKS = O_TILES * CHUNKS
 Z_O_TILE = 2
 
 FLOPS = 2 * OUT_CHANNELS * CHANNELS * UP_POSITIONS
@@ -57,29 +62,37 @@ def tile_upconvcropcat_k_kernel(tc, x, z, W, b, out):
 
     with ExitStack() as stack:
         const = stack.enter_context(tc.tile_pool(name="const", bufs=1))
-        x_raw_pool = stack.enter_context(tc.tile_pool(name="x_raw", bufs=CHUNKS))
-        w_raw_pool = stack.enter_context(tc.tile_pool(name="w_raw", bufs=O_TILES * CHUNKS))
+        x_raw_pool = stack.enter_context(tc.tile_pool(name="x_raw", bufs=PIECES))
+        w_raw_pool = stack.enter_context(tc.tile_pool(name="w_raw", bufs=O_TILES * PIECES))
         z_raw_pool = stack.enter_context(tc.tile_pool(name="z_raw", bufs=Z_TILES))
-        x_mx_pool = stack.enter_context(tc.tile_pool(name="x_mx", bufs=CHUNKS))
-        stage = stack.enter_context(tc.tile_pool(name="stage", bufs=3))
-        results = stack.enter_context(tc.tile_pool(name="results", bufs=2))
+        x_mx_pool = stack.enter_context(tc.tile_pool(name="x_mx", bufs=PIECES))
+        stage = stack.enter_context(tc.tile_pool(name="stage", bufs=3 * RUN_PIECES))
+        results = stack.enter_context(tc.tile_pool(name="results", bufs=4))
         acc_pool = stack.enter_context(tc.psum_pool(name="acc", bufs=GROUPS))
-        turned_pool = stack.enter_context(tc.psum_pool(name="turned", bufs=TRANSPOSE_BANKS))
+        turned_pool = stack.enter_context(tc.psum_pool(name="turned", bufs=PSUM_BANKS - GROUPS))
         stack.enter_context(tc.manual_schedule())
 
-        def load_w(q):
-            m, n = divmod(q, CHUNKS)
-            w_raw = w_raw_pool.tile([P, CHUNK_K], BF16)
-            nc.sync.dma_start(out=w_raw[:], in_=W[m * P : (m + 1) * P, n * CHUNK_K : (n + 1) * CHUNK_K])
-            return w_raw
+        x_raws = []
+        w_raws = []
+        z_raws = []
 
-        def load_x(n):
-            x_raw = x_raw_pool.tile([P, CHUNK_K], BF16)
-            nc.sync.dma_start(
-                out=x_raw[:].rearrange("p (s f) -> p s f", f=PAIR * POSITIONS),
-                in_=x_rows[n * CHUNK_K : (n + 1) * CHUNK_K, :].rearrange("(s q e) w -> q s (e w)", q=P, e=PAIR),
-            )
-            return x_raw
+        def load_w_chunk(q):
+            m, n = divmod(q, CHUNKS)
+            for piece in range(n * RUN_PIECES, (n + 1) * RUN_PIECES):
+                w_raw = w_raw_pool.tile([P, PIECE_K], BF16)
+                nc.sync.dma_start(out=w_raw[:], in_=W[m * P : (m + 1) * P, piece * PIECE_K : (piece + 1) * PIECE_K])
+                w_raws.append(w_raw)
+
+        def load_x_chunk(n):
+            for piece in range(n * RUN_PIECES, (n + 1) * RUN_PIECES):
+                x_raw = x_raw_pool.tile([P, PIECE_K], BF16)
+                nc.sync.dma_start(
+                    out=x_raw[:].rearrange("p (s f) -> p s f", f=PAIR * POSITIONS),
+                    in_=x_rows[piece * PIECE_K : (piece + 1) * PIECE_K, :].rearrange(
+                        "(s q e) w -> q s (e w)", q=P, e=PAIR
+                    ),
+                )
+                x_raws.append(x_raw)
 
         def load_z(i):
             z_raw = z_raw_pool.tile([P, UP * DEPTH * Z_HEIGHT * Z_WIDTH], BF16)
@@ -87,125 +100,112 @@ def tile_upconvcropcat_k_kernel(tc, x, z, W, b, out):
                 out=z_raw[:],
                 in_=z_rows[i * P : (i + 1) * P, MARGIN : MARGIN + UP * DEPTH, :].rearrange("c d f -> c (d f)"),
             )
-            return z_raw
+            z_raws.append(z_raw)
 
-        x_raws = []
-        w_raws = []
-        z_raws = []
-        for n in range(CHUNKS):
-            x_raws.append(load_x(n))
-            w_raws.append(load_w(n))
-        for q in range(CHUNKS, (O_TILES - 1) * CHUNKS):
-            w_raws.append(load_w(q))
-        for i in range(Z_TILES):
-            z_raws.append(load_z(i))
-        for q in range((O_TILES - 1) * CHUNKS, O_TILES * CHUNKS):
-            w_raws.append(load_w(q))
+        load_w_chunk(0)
+        load_w_chunk(1)
+        for q in range(ALL_CHUNKS - 2):
+            if q < CHUNKS:
+                load_x_chunk(q)
+            if q + 2 == (O_TILES - 1) * CHUNKS:
+                for i in range(Z_TILES):
+                    load_z(i)
+            load_w_chunk(q + 2)
 
         identity = const.tile([P, P], F32)
         make_identity(nc, identity[:])
 
-        b_rows = const.tile([P, P], BF16)
-        nc.vector.memset(b_rows[:], 0.0)
-        nc.scalar.dma_start(out=b_rows[0:O_TILES, :], in_=b.rearrange("(m o) -> m o", m=O_TILES))
-        b_rows_f32 = const.tile([P, P], F32)
-        nc.vector.tensor_copy(out=b_rows_f32[:], in_=b_rows[:])
-        b_turned = turned_pool.tile([P, BANK_WORDS], F32, tag="turned")
-        nc.tensor.transpose(out=b_turned[:, 0:P], in_=b_rows_f32[:], identity=identity[:])
-        bias = const.tile([P, O_TILES], F32)
-        nc.scalar.activation(out=bias[:], in_=b_turned[:, 0:O_TILES], func=IDENTITY)
+        def transpose_chunk(q):
+            banks = []
+            for w_raw in w_raws[q * RUN_PIECES : (q + 1) * RUN_PIECES]:
+                raw_words = w_raw[:].bitcast(F32)
+                for h in range(PIECE_BANKS):
+                    turned = turned_pool.tile([P, BANK_WORDS], F32, tag="turned")
+                    for s in range(BANK_WORDS // P):
+                        nc.tensor.transpose(
+                            out=turned[:, s * P : (s + 1) * P],
+                            in_=raw_words[:, h * BANK_WORDS + s * P : h * BANK_WORDS + (s + 1) * P],
+                            identity=identity[:],
+                        )
+                    banks.append(turned)
+            return banks
 
-        x_words = []
-        x_scales = []
+        def quantise_chunk(banks):
+            grouped = []
+            for i in range(RUN_PIECES):
+                w_grouped = stage.tile([P, PIECE_K], BF16, align_bytes=64)
+                grouped_words = w_grouped[:].bitcast(F32)
+                for h in range(PIECE_BANKS):
+                    copy = nc.scalar.copy if h == 0 else nc.vector.tensor_copy
+                    copy(
+                        out=grouped_words[:, h * BANK_WORDS : (h + 1) * BANK_WORDS].rearrange(
+                            "p (g o u) -> p g o u", g=BANK_PASSES, u=PAIR
+                        ),
+                        in_=banks[i * PIECE_BANKS + h][:].rearrange("p (g u o) -> p g o u", g=BANK_PASSES, u=PAIR),
+                    )
+                grouped.append(w_grouped)
+            quantised = []
+            for w_grouped in grouped:
+                w_words = stage.tile([P, PIECE_PASSES * P], U32, align_bytes=64)
+                w_scales = stage.tile([P, PIECE_PASSES * P], U8, align_bytes=64)
+                nc.vector.quantize_mx(out=w_words[:].bitcast(FP8X4), scales=w_scales[:], in_=w_grouped[:])
+                quantised.append((w_words, w_scales))
+            return quantised
 
-        def regroup_x(n):
-            x_grouped = stage.tile([P, CHUNK_K], BF16, align_bytes=64)
-            for g in range(CHUNK_PASSES):
+        x_quantised = []
+
+        def prepare_x(piece):
+            x_grouped = stage.tile([P, PIECE_K], BF16, align_bytes=64)
+            for g in range(PIECE_PASSES):
                 cols = slice(g * K_PASS, (g + 1) * K_PASS)
                 copy = nc.vector.tensor_copy if g % 2 == 0 else nc.scalar.copy
                 copy(
                     out=x_grouped[:, cols].rearrange("p (c i t) -> p c t i", i=4, t=PACK),
-                    in_=x_raws[n][:, cols].rearrange("p (t c i) -> p c t i", t=PACK, i=4),
+                    in_=x_raws[piece][:, cols].rearrange("p (t c i) -> p c t i", t=PACK, i=4),
                 )
-            return x_grouped
-
-        def quantise_x(x_grouped):
-            words = x_mx_pool.tile([P, CHUNK_PASSES * N_MOVING], U32, align_bytes=64)
-            scales = x_mx_pool.tile([P, CHUNK_PASSES * N_MOVING], U8, align_bytes=64)
-            for g in range(CHUNK_PASSES):
+            x_words = x_mx_pool.tile([P, PIECE_PASSES * N_MOVING], U32, align_bytes=64)
+            x_scales = x_mx_pool.tile([P, PIECE_PASSES * N_MOVING], U8, align_bytes=64)
+            for g in range(PIECE_PASSES):
                 for r in range(UP):
                     cols = slice(g * N_MOVING + r * POSITIONS, g * N_MOVING + (r + 1) * POSITIONS)
                     nc.vector.quantize_mx(
-                        out=words[:, cols].bitcast(FP8X4),
-                        scales=scales[:, cols],
+                        out=x_words[:, cols].bitcast(FP8X4),
+                        scales=x_scales[:, cols],
                         in_=x_grouped[:, g * K_PASS : (g + 1) * K_PASS],
                     )
-            x_words.append(words)
-            x_scales.append(scales)
+            x_quantised.append((x_words, x_scales))
 
-        def transpose_w(q):
-            raw_words = w_raws[q][:].bitcast(F32)
-            w_grouped = stage.tile([P, CHUNK_K], BF16, align_bytes=64)
-            grouped_words = w_grouped[:].bitcast(F32)
-            for h in range(CHUNK_BANKS):
-                turned = turned_pool.tile([P, BANK_WORDS], F32, tag="turned")
-                for s in range(BANK_WORDS // P):
-                    nc.tensor.transpose(
-                        out=turned[:, s * P : (s + 1) * P],
-                        in_=raw_words[:, h * BANK_WORDS + s * P : h * BANK_WORDS + (s + 1) * P],
-                        identity=identity[:],
-                    )
-                nc.scalar.copy(
-                    out=grouped_words[:, h * BANK_WORDS : (h + 1) * BANK_WORDS].rearrange(
-                        "p (g o u) -> p g o u", g=BANK_PASSES, u=PAIR
-                    ),
-                    in_=turned[:].rearrange("p (g u o) -> p g o u", g=BANK_PASSES, u=PAIR),
-                )
-            return w_grouped
-
-        def quantise_w(w_grouped):
-            words = stage.tile([P, CHUNK_PASSES * P], U32, align_bytes=64)
-            scales = stage.tile([P, CHUNK_PASSES * P], U8, align_bytes=64)
-            nc.vector.quantize_mx(out=words[:].bitcast(FP8X4), scales=scales[:], in_=w_grouped[:])
-            return words, scales
-
-        def prepare(q):
-            if q < CHUNKS:
-                x_grouped = regroup_x(q)
-            w_grouped = transpose_w(q)
-            if q < CHUNKS:
-                quantise_x(x_grouped)
-            return quantise_w(w_grouped)
-
-        def multiply(n, w_words, w_scales, acc):
-            for g in range(CHUNK_PASSES):
-                c = n * CHUNK_PASSES + g
-                o_cols = slice(g * P, (g + 1) * P)
-                x_cols = slice(g * N_MOVING, (g + 1) * N_MOVING)
-                for group in acc:
-                    nc.tensor.matmul_mx(
-                        out=group[:],
-                        lhsT=w_words[:, o_cols].bitcast(FP8X4),
-                        lhsT_scale=w_scales[:, o_cols],
-                        rhs=x_words[n][:, x_cols].bitcast(FP8X4),
-                        rhs_scale=x_scales[n][:, x_cols],
-                        start=(c == 0),
-                        stop=(c == PASSES - 1),
-                    )
+        def multiply(n, quantised, acc):
+            for i in range(RUN_PIECES):
+                w_words, w_scales = quantised[i]
+                x_words, x_scales = x_quantised[n * RUN_PIECES + i]
+                for g in range(PIECE_PASSES):
+                    c = (n * RUN_PIECES + i) * PIECE_PASSES + g
+                    o_cols = slice(g * P, (g + 1) * P)
+                    x_cols = slice(g * N_MOVING, (g + 1) * N_MOVING)
+                    for group in acc:
+                        nc.tensor.matmul_mx(
+                            out=group[:],
+                            lhsT=w_words[:, o_cols].bitcast(FP8X4),
+                            lhsT_scale=w_scales[:, o_cols],
+                            rhs=x_words[:, x_cols].bitcast(FP8X4),
+                            rhs_scale=x_scales[:, x_cols],
+                            start=(c == 0),
+                            stop=(c == PASSES - 1),
+                        )
 
         def finish(m, acc):
-            y = results.tile([P, UP_POSITIONS], F32)
-            y_view = y[:].rearrange(
-                "p (i a h b k r) -> p a b i h k r", i=DEPTH, a=UP, h=HEIGHT, b=UP, k=WIDTH, r=UP
-            )
-            for j in range(GROUPS):
-                y_part = y_view[:, j // UP, j % UP]
-                sums = acc[j][:].rearrange("p (r i h k) -> p i h k r", r=UP, i=DEPTH, h=HEIGHT)
-                if j % 2 == 0:
-                    nc.scalar.activation(out=y_part, in_=sums, func=IDENTITY, bias=bias[:, m : m + 1])
-                else:
-                    nc.vector.tensor_scalar_add(out=y_part, in0=sums, scalar1=bias[:, m : m + 1])
-            nc.sync.dma_start(out=out_rows[m * P : (m + 1) * P, :], in_=y[:])
+            planes = out_rows[m * P : (m + 1) * P, :].rearrange("o (i a f) -> o a i f", i=DEPTH, a=UP)
+            for a in range(UP):
+                y = results.tile([P, DEPTH * UP_PLANE], F32)
+                y_view = y[:].rearrange("p (i h b k r) -> p b i h k r", i=DEPTH, h=HEIGHT, b=UP, k=WIDTH, r=UP)
+                for bb in range(UP):
+                    sums = acc[a * UP + bb][:].rearrange("p (r i h k) -> p i h k r", r=UP, i=DEPTH, h=HEIGHT)
+                    if bb == 0:
+                        nc.scalar.activation(out=y_view[:, bb], in_=sums, func=IDENTITY, bias=bias[:, m : m + 1])
+                    else:
+                        nc.vector.tensor_scalar_add(out=y_view[:, bb], in0=sums, scalar1=bias[:, m : m + 1])
+                nc.sync.dma_start(out=planes[:, a], in_=y[:].rearrange("p (i f) -> p i f", i=DEPTH))
 
         def crop_z(i):
             cropped = results.tile([P, UP_POSITIONS], F32)
@@ -217,20 +217,38 @@ def tile_upconvcropcat_k_kernel(tc, x, z, W, b, out):
             )
             nc.sync.dma_start(out=out_rows[OUT_CHANNELS + i * P : OUT_CHANNELS + (i + 1) * P, :], in_=cropped[:])
 
-        ready = prepare(0)
+        b_rows = const.tile([P, P], BF16)
+        nc.vector.memset(b_rows[:], 0.0)
+        nc.scalar.dma_start(out=b_rows[0:O_TILES, :], in_=b.rearrange("(m o) -> m o", m=O_TILES))
+        b_rows_f32 = const.tile([P, P], F32)
+        nc.vector.tensor_copy(out=b_rows_f32[:], in_=b_rows[:])
+
+        ready = quantise_chunk(transpose_chunk(0))
+
+        b_turned = turned_pool.tile([P, BANK_WORDS], F32, tag="turned")
+        nc.tensor.transpose(out=b_turned[:, 0:P], in_=b_rows_f32[:], identity=identity[:])
+        bias = const.tile([P, O_TILES], F32)
+        nc.scalar.activation(out=bias[:], in_=b_turned[:, 0:O_TILES], func=IDENTITY)
+
         acc = []
-        for q in range(O_TILES * CHUNKS):
+        for q in range(ALL_CHUNKS):
             m, n = divmod(q, CHUNKS)
-            w_words, w_scales = ready
-            if q + 1 < O_TILES * CHUNKS:
-                ready = prepare(q + 1)
+            quantised = ready
+            if q + 1 < ALL_CHUNKS:
+                banks = transpose_chunk(q + 1)
+            if m == 0:
+                for piece in range(n * RUN_PIECES, (n + 1) * RUN_PIECES):
+                    prepare_x(piece)
+            if q + 1 < ALL_CHUNKS:
+                ready = quantise_chunk(banks)
             if n == 0:
                 acc = []
                 for j in range(GROUPS):
                     group = acc_pool.tile([P, N_MOVING], F32)
                     acc.append(group)
-            multiply(n, w_words, w_scales, acc)
+            multiply(n, quantised, acc)
             if m == Z_O_TILE:
-                crop_z(n)
+                for i in range(n * Z_TILES // CHUNKS, (n + 1) * Z_TILES // CHUNKS):
+                    crop_z(i)
             if n == CHUNKS - 1:
                 finish(m, acc)

@@ -43,8 +43,13 @@ PIECES = PASSES // PIECE_PASSES
 PIECE_BANKS = PIECE_K // PAIR // BANK_WORDS
 BANK_PASSES = PIECE_PASSES // PIECE_BANKS
 RUN_PIECES = (PSUM_BANKS - GROUPS) // PIECE_BANKS
+CHUNK_PASSES = RUN_PIECES * PIECE_PASSES
 CHUNKS = PIECES // RUN_PIECES
 ALL_CHUNKS = O_TILES * CHUNKS
+X_PIECE_PASSES = 2
+X_PIECE_K = X_PIECE_PASSES * K_PASS
+X_PIECES = PASSES // X_PIECE_PASSES
+CHUNK_X_PIECES = CHUNK_PASSES // X_PIECE_PASSES
 Z_O_TILE = 2
 
 FLOPS = 2 * OUT_CHANNELS * CHANNELS * UP_POSITIONS
@@ -62,10 +67,11 @@ def tile_upconvcropcat_k_kernel(tc, x, z, W, b, out):
 
     with ExitStack() as stack:
         const = stack.enter_context(tc.tile_pool(name="const", bufs=1))
-        x_raw_pool = stack.enter_context(tc.tile_pool(name="x_raw", bufs=PIECES))
+        x_raw_pool = stack.enter_context(tc.tile_pool(name="x_raw", bufs=X_PIECES))
         w_raw_pool = stack.enter_context(tc.tile_pool(name="w_raw", bufs=O_TILES * PIECES))
         z_raw_pool = stack.enter_context(tc.tile_pool(name="z_raw", bufs=Z_TILES))
-        x_mx_pool = stack.enter_context(tc.tile_pool(name="x_mx", bufs=PIECES))
+        x_mx_pool = stack.enter_context(tc.tile_pool(name="x_mx", bufs=X_PIECES))
+        x_stage = stack.enter_context(tc.tile_pool(name="x_stage", bufs=3))
         stage = stack.enter_context(tc.tile_pool(name="stage", bufs=3 * RUN_PIECES))
         results = stack.enter_context(tc.tile_pool(name="results", bufs=4))
         acc_pool = stack.enter_context(tc.psum_pool(name="acc", bufs=GROUPS))
@@ -84,12 +90,12 @@ def tile_upconvcropcat_k_kernel(tc, x, z, W, b, out):
                 w_raws.append(w_raw)
 
         def load_x_chunk(n):
-            for piece in range(n * RUN_PIECES, (n + 1) * RUN_PIECES):
-                x_raw = x_raw_pool.tile([P, PIECE_K], BF16)
+            for x_piece in range(n * CHUNK_X_PIECES, (n + 1) * CHUNK_X_PIECES):
+                x_raw = x_raw_pool.tile([P, X_PIECE_K], BF16)
                 nc.sync.dma_start(
                     out=x_raw[:].rearrange("p (s f) -> p s f", f=PAIR * POSITIONS),
-                    in_=x_rows[piece * PIECE_K : (piece + 1) * PIECE_K, :].rearrange(
-                        "(s q e) w -> q s (e w)", q=P, e=PAIR
+                    in_=x_rows[x_piece * X_PIECE_K : (x_piece + 1) * X_PIECE_K, :].rearrange(
+                        "(s p e) w -> p s (e w)", p=P, e=PAIR
                     ),
                 )
                 x_raws.append(x_raw)
@@ -131,41 +137,38 @@ def tile_upconvcropcat_k_kernel(tc, x, z, W, b, out):
             return banks
 
         def quantise_chunk(banks):
-            grouped = []
+            w_passes = []
             for i in range(RUN_PIECES):
                 w_grouped = stage.tile([P, PIECE_K], BF16, align_bytes=64)
                 grouped_words = w_grouped[:].bitcast(F32)
                 for h in range(PIECE_BANKS):
-                    copy = nc.scalar.copy if h == 0 else nc.vector.tensor_copy
-                    copy(
+                    nc.scalar.copy(
                         out=grouped_words[:, h * BANK_WORDS : (h + 1) * BANK_WORDS].rearrange(
                             "p (g o u) -> p g o u", g=BANK_PASSES, u=PAIR
                         ),
                         in_=banks[i * PIECE_BANKS + h][:].rearrange("p (g u o) -> p g o u", g=BANK_PASSES, u=PAIR),
                     )
-                grouped.append(w_grouped)
-            quantised = []
-            for w_grouped in grouped:
                 w_words = stage.tile([P, PIECE_PASSES * P], U32, align_bytes=64)
                 w_scales = stage.tile([P, PIECE_PASSES * P], U8, align_bytes=64)
                 nc.vector.quantize_mx(out=w_words[:].bitcast(FP8X4), scales=w_scales[:], in_=w_grouped[:])
-                quantised.append((w_words, w_scales))
-            return quantised
+                for g in range(PIECE_PASSES):
+                    w_passes.append((w_words[:, g * P : (g + 1) * P], w_scales[:, g * P : (g + 1) * P]))
+            return w_passes
 
-        x_quantised = []
+        x_passes = []
 
-        def prepare_x(piece):
-            x_grouped = stage.tile([P, PIECE_K], BF16, align_bytes=64)
-            for g in range(PIECE_PASSES):
+        def prepare_x(x_piece):
+            x_grouped = x_stage.tile([P, X_PIECE_K], BF16, align_bytes=64)
+            for g in range(X_PIECE_PASSES):
                 cols = slice(g * K_PASS, (g + 1) * K_PASS)
-                copy = nc.vector.tensor_copy if g % 2 == 0 else nc.scalar.copy
+                copy = nc.vector.tensor_copy if g == 0 else nc.scalar.copy
                 copy(
                     out=x_grouped[:, cols].rearrange("p (c i t) -> p c t i", i=4, t=PACK),
-                    in_=x_raws[piece][:, cols].rearrange("p (t c i) -> p c t i", t=PACK, i=4),
+                    in_=x_raws[x_piece][:, cols].rearrange("p (t c i) -> p c t i", t=PACK, i=4),
                 )
-            x_words = x_mx_pool.tile([P, PIECE_PASSES * N_MOVING], U32, align_bytes=64)
-            x_scales = x_mx_pool.tile([P, PIECE_PASSES * N_MOVING], U8, align_bytes=64)
-            for g in range(PIECE_PASSES):
+            x_words = x_mx_pool.tile([P, X_PIECE_PASSES * N_MOVING], U32, align_bytes=64)
+            x_scales = x_mx_pool.tile([P, X_PIECE_PASSES * N_MOVING], U8, align_bytes=64)
+            for g in range(X_PIECE_PASSES):
                 for r in range(UP):
                     cols = slice(g * N_MOVING + r * POSITIONS, g * N_MOVING + (r + 1) * POSITIONS)
                     nc.vector.quantize_mx(
@@ -173,26 +176,24 @@ def tile_upconvcropcat_k_kernel(tc, x, z, W, b, out):
                         scales=x_scales[:, cols],
                         in_=x_grouped[:, g * K_PASS : (g + 1) * K_PASS],
                     )
-            x_quantised.append((x_words, x_scales))
+                cols = slice(g * N_MOVING, (g + 1) * N_MOVING)
+                x_passes.append((x_words[:, cols], x_scales[:, cols]))
 
-        def multiply(n, quantised, acc):
-            for i in range(RUN_PIECES):
-                w_words, w_scales = quantised[i]
-                x_words, x_scales = x_quantised[n * RUN_PIECES + i]
-                for g in range(PIECE_PASSES):
-                    c = (n * RUN_PIECES + i) * PIECE_PASSES + g
-                    o_cols = slice(g * P, (g + 1) * P)
-                    x_cols = slice(g * N_MOVING, (g + 1) * N_MOVING)
-                    for group in acc:
-                        nc.tensor.matmul_mx(
-                            out=group[:],
-                            lhsT=w_words[:, o_cols].bitcast(FP8X4),
-                            lhsT_scale=w_scales[:, o_cols],
-                            rhs=x_words[:, x_cols].bitcast(FP8X4),
-                            rhs_scale=x_scales[:, x_cols],
-                            start=(c == 0),
-                            stop=(c == PASSES - 1),
-                        )
+        def multiply(n, w_passes, acc):
+            for g in range(CHUNK_PASSES):
+                c = n * CHUNK_PASSES + g
+                w_words, w_scales = w_passes[g]
+                x_words, x_scales = x_passes[c]
+                for group in acc:
+                    nc.tensor.matmul_mx(
+                        out=group[:],
+                        lhsT=w_words.bitcast(FP8X4),
+                        lhsT_scale=w_scales,
+                        rhs=x_words.bitcast(FP8X4),
+                        rhs_scale=x_scales,
+                        start=(c == 0),
+                        stop=(c == PASSES - 1),
+                    )
 
         def finish(m, acc):
             planes = out_rows[m * P : (m + 1) * P, :].rearrange("o (i a f) -> o a i f", i=DEPTH, a=UP)
@@ -221,7 +222,7 @@ def tile_upconvcropcat_k_kernel(tc, x, z, W, b, out):
         nc.vector.memset(b_rows[:], 0.0)
         nc.scalar.dma_start(out=b_rows[0:O_TILES, :], in_=b.rearrange("(m o) -> m o", m=O_TILES))
         b_rows_f32 = const.tile([P, P], F32)
-        nc.vector.tensor_copy(out=b_rows_f32[:], in_=b_rows[:])
+        nc.scalar.activation(out=b_rows_f32[:], in_=b_rows[:], func=IDENTITY)
 
         ready = quantise_chunk(transpose_chunk(0))
 
@@ -233,12 +234,12 @@ def tile_upconvcropcat_k_kernel(tc, x, z, W, b, out):
         acc = []
         for q in range(ALL_CHUNKS):
             m, n = divmod(q, CHUNKS)
-            quantised = ready
+            w_passes = ready
             if q + 1 < ALL_CHUNKS:
                 banks = transpose_chunk(q + 1)
             if m == 0:
-                for piece in range(n * RUN_PIECES, (n + 1) * RUN_PIECES):
-                    prepare_x(piece)
+                for x_piece in range(n * CHUNK_X_PIECES, (n + 1) * CHUNK_X_PIECES):
+                    prepare_x(x_piece)
             if q + 1 < ALL_CHUNKS:
                 ready = quantise_chunk(banks)
             if n == 0:
@@ -246,7 +247,7 @@ def tile_upconvcropcat_k_kernel(tc, x, z, W, b, out):
                 for j in range(GROUPS):
                     group = acc_pool.tile([P, N_MOVING], F32)
                     acc.append(group)
-            multiply(n, quantised, acc)
+            multiply(n, w_passes, acc)
             if m == Z_O_TILE:
                 for i in range(n * Z_TILES // CHUNKS, (n + 1) * Z_TILES // CHUNKS):
                     crop_z(i)

from contextlib import ExitStack

import concourse.mybir as mybir
from concourse.masks import make_identity

F32 = mybir.dt.float32
BF16 = mybir.dt.bfloat16
U32 = mybir.dt.uint32
U8 = mybir.dt.uint8
FP8X4 = mybir.dt.float8_e4m3fn_x4
IDENTITY = mybir.ActivationFunctionType.Identity

P = 128
PACK = 4
K_PASS = P * PACK
PAIR = 2
BANK_WORDS = 512
PSUM_BANKS = 8

CHANNELS = 8192
OUT_CHANNELS = 512
Z_CHANNELS = 512
DEPTH = 2
HEIGHT = 4
WIDTH = 16
POSITIONS = DEPTH * HEIGHT * WIDTH
UP = 2
UP_PLANE = UP * HEIGHT * UP * WIDTH
UP_POSITIONS = UP * DEPTH * UP_PLANE
MARGIN = 2
Z_HEIGHT = UP * HEIGHT + 2 * MARGIN
Z_WIDTH = UP * WIDTH + 2 * MARGIN

PASSES = CHANNELS // K_PASS
O_TILES = OUT_CHANNELS // P
Z_TILES = Z_CHANNELS // P
N_MOVING = UP * POSITIONS
GROUPS = UP * UP

PIECE_PASSES = 4
PIECE_K = PIECE_PASSES * K_PASS
PIECES = PASSES // PIECE_PASSES
PIECE_BANKS = PIECE_K // PAIR // BANK_WORDS
BANK_PASSES = PIECE_PASSES // PIECE_BANKS
RUN_PIECES = (PSUM_BANKS - GROUPS) // PIECE_BANKS
CHUNK_PASSES = RUN_PIECES * PIECE_PASSES
CHUNKS = PIECES // RUN_PIECES
ALL_CHUNKS = O_TILES * CHUNKS
X_PIECE_PASSES = 2
X_PIECE_K = X_PIECE_PASSES * K_PASS
X_PIECES = PASSES // X_PIECE_PASSES
CHUNK_X_PIECES = CHUNK_PASSES // X_PIECE_PASSES
Z_O_TILE = 2

FLOPS = 2 * OUT_CHANNELS * CHANNELS * UP_POSITIONS
BYTES = (
    2 * (CHANNELS * POSITIONS + OUT_CHANNELS * CHANNELS + OUT_CHANNELS + Z_CHANNELS * UP_POSITIONS)
    + 4 * (OUT_CHANNELS + Z_CHANNELS) * UP_POSITIONS
)


def tile_upconvcropcat_k_kernel(tc, x, z, W, b, out):
    nc = tc.nc
    x_rows = x.rearrange("n c d h w -> (n c) (d h w)")
    z_rows = z.rearrange("n c d h w -> (n c) d (h w)")
    out_rows = out.rearrange("n c d h w -> (n c) (d h w)")

    with ExitStack() as stack:
        const = stack.enter_context(tc.tile_pool(name="const", bufs=1))
        x_raw_pool = stack.enter_context(tc.tile_pool(name="x_raw", bufs=X_PIECES))
        w_raw_pool = stack.enter_context(tc.tile_pool(name="w_raw", bufs=O_TILES * PIECES))
        z_raw_pool = stack.enter_context(tc.tile_pool(name="z_raw", bufs=Z_TILES))
        x_mx_pool = stack.enter_context(tc.tile_pool(name="x_mx", bufs=X_PIECES))
        x_stage = stack.enter_context(tc.tile_pool(name="x_stage", bufs=3))
        stage = stack.enter_context(tc.tile_pool(name="stage", bufs=3 * RUN_PIECES))
        results = stack.enter_context(tc.tile_pool(name="results", bufs=4))
        acc_pool = stack.enter_context(tc.psum_pool(name="acc", bufs=GROUPS))
        turned_pool = stack.enter_context(tc.psum_pool(name="turned", bufs=PSUM_BANKS - GROUPS))
        stack.enter_context(tc.manual_schedule())

        x_raws = []
        w_raws = []
        z_raws = []

        def load_w_chunk(q):
            m, n = divmod(q, CHUNKS)
            for piece in range(n * RUN_PIECES, (n + 1) * RUN_PIECES):
                w_raw = w_raw_pool.tile([P, PIECE_K], BF16)
                nc.sync.dma_start(out=w_raw[:], in_=W[m * P : (m + 1) * P, piece * PIECE_K : (piece + 1) * PIECE_K])
                w_raws.append(w_raw)

        def load_x_chunk(n):
            for x_piece in range(n * CHUNK_X_PIECES, (n + 1) * CHUNK_X_PIECES):
                x_raw = x_raw_pool.tile([P, X_PIECE_K], BF16)
                nc.sync.dma_start(
                    out=x_raw[:].rearrange("p (s f) -> p s f", f=PAIR * POSITIONS),
                    in_=x_rows[x_piece * X_PIECE_K : (x_piece + 1) * X_PIECE_K, :].rearrange(
                        "(s p e) w -> p s (e w)", p=P, e=PAIR
                    ),
                )
                x_raws.append(x_raw)

        def load_z(i):
            z_raw = z_raw_pool.tile([P, UP * DEPTH * Z_HEIGHT * Z_WIDTH], BF16)
            nc.sync.dma_start(
                out=z_raw[:],
                in_=z_rows[i * P : (i + 1) * P, MARGIN : MARGIN + UP * DEPTH, :].rearrange("c d f -> c (d f)"),
            )
            z_raws.append(z_raw)

        load_w_chunk(0)
        load_w_chunk(1)
        for q in range(ALL_CHUNKS - 2):
            if q < CHUNKS:
                load_x_chunk(q)
            if q + 2 == (O_TILES - 1) * CHUNKS:
                for i in range(Z_TILES):
                    load_z(i)
            load_w_chunk(q + 2)

        identity = const.tile([P, P], F32)
        make_identity(nc, identity[:])

        def transpose_chunk(q):
            banks = []
            for w_raw in w_raws[q * RUN_PIECES : (q + 1) * RUN_PIECES]:
                raw_words = w_raw[:].bitcast(F32)
                for h in range(PIECE_BANKS):
                    turned = turned_pool.tile([P, BANK_WORDS], F32, tag="turned")
                    for s in range(BANK_WORDS // P):
                        nc.tensor.transpose(
                            out=turned[:, s * P : (s + 1) * P],
                            in_=raw_words[:, h * BANK_WORDS + s * P : h * BANK_WORDS + (s + 1) * P],
                            identity=identity[:],
                        )
                    banks.append(turned)
            return banks

        def quantise_chunk(banks):
            w_passes = []
            for i in range(RUN_PIECES):
                w_grouped = stage.tile([P, PIECE_K], BF16, align_bytes=64)
                grouped_words = w_grouped[:].bitcast(F32)
                for h in range(PIECE_BANKS):
                    nc.scalar.copy(
                        out=grouped_words[:, h * BANK_WORDS : (h + 1) * BANK_WORDS].rearrange(
                            "p (g o u) -> p g o u", g=BANK_PASSES, u=PAIR
                        ),
                        in_=banks[i * PIECE_BANKS + h][:].rearrange("p (g u o) -> p g o u", g=BANK_PASSES, u=PAIR),
                    )
                w_words = stage.tile([P, PIECE_PASSES * P], U32, align_bytes=64)
                w_scales = stage.tile([P, PIECE_PASSES * P], U8, align_bytes=64)
                nc.vector.quantize_mx(out=w_words[:].bitcast(FP8X4), scales=w_scales[:], in_=w_grouped[:])
                for g in range(PIECE_PASSES):
                    w_passes.append((w_words[:, g * P : (g + 1) * P], w_scales[:, g * P : (g + 1) * P]))
            return w_passes

        x_passes = []

        def prepare_x(x_piece):
            x_grouped = x_stage.tile([P, X_PIECE_K], BF16, align_bytes=64)
            for g in range(X_PIECE_PASSES):
                cols = slice(g * K_PASS, (g + 1) * K_PASS)
                copy = nc.vector.tensor_copy if g == 0 else nc.scalar.copy
                copy(
                    out=x_grouped[:, cols].rearrange("p (c i t) -> p c t i", i=4, t=PACK),
                    in_=x_raws[x_piece][:, cols].rearrange("p (t c i) -> p c t i", t=PACK, i=4),
                )
            x_words = x_mx_pool.tile([P, X_PIECE_PASSES * N_MOVING], U32, align_bytes=64)
            x_scales = x_mx_pool.tile([P, X_PIECE_PASSES * N_MOVING], U8, align_bytes=64)
            for g in range(X_PIECE_PASSES):
                for r in range(UP):
                    cols = slice(g * N_MOVING + r * POSITIONS, g * N_MOVING + (r + 1) * POSITIONS)
                    nc.vector.quantize_mx(
                        out=x_words[:, cols].bitcast(FP8X4),
                        scales=x_scales[:, cols],
                        in_=x_grouped[:, g * K_PASS : (g + 1) * K_PASS],
                    )
                cols = slice(g * N_MOVING, (g + 1) * N_MOVING)
                x_passes.append((x_words[:, cols], x_scales[:, cols]))

        def multiply(n, w_passes, acc):
            for g in range(CHUNK_PASSES):
                c = n * CHUNK_PASSES + g
                w_words, w_scales = w_passes[g]
                x_words, x_scales = x_passes[c]
                for group in acc:
                    nc.tensor.matmul_mx(
                        out=group[:],
                        lhsT=w_words.bitcast(FP8X4),
                        lhsT_scale=w_scales,
                        rhs=x_words.bitcast(FP8X4),
                        rhs_scale=x_scales,
                        start=(c == 0),
                        stop=(c == PASSES - 1),
                    )

        def finish(m, acc):
            planes = out_rows[m * P : (m + 1) * P, :].rearrange("o (i a f) -> o a i f", i=DEPTH, a=UP)
            for a in range(UP):
                y = results.tile([P, DEPTH * UP_PLANE], F32)
                y_view = y[:].rearrange("p (i h b k r) -> p b i h k r", i=DEPTH, h=HEIGHT, b=UP, k=WIDTH, r=UP)
                for bb in range(UP):
                    sums = acc[a * UP + bb][:].rearrange("p (r i h k) -> p i h k r", r=UP, i=DEPTH, h=HEIGHT)
                    if bb == 0:
                        nc.scalar.activation(out=y_view[:, bb], in_=sums, func=IDENTITY, bias=bias[:, m : m + 1])
                    else:
                        nc.vector.tensor_scalar_add(out=y_view[:, bb], in0=sums, scalar1=bias[:, m : m + 1])
                nc.sync.dma_start(out=planes[:, a], in_=y[:].rearrange("p (i f) -> p i f", i=DEPTH))

        def crop_z(i):
            cropped = results.tile([P, UP_POSITIONS], F32)
            nc.vector.tensor_copy(
                out=cropped[:].rearrange("p (d h w) -> p d h w", h=UP * HEIGHT, w=UP * WIDTH),
                in_=z_raws[i][:].rearrange("p (d h w) -> p d h w", h=Z_HEIGHT, w=Z_WIDTH)[
                    :, :, MARGIN : MARGIN + UP * HEIGHT, MARGIN : MARGIN + UP * WIDTH
                ],
            )
            nc.sync.dma_start(out=out_rows[OUT_CHANNELS + i * P : OUT_CHANNELS + (i + 1) * P, :], in_=cropped[:])

        b_rows = const.tile([P, P], BF16)
        nc.vector.memset(b_rows[:], 0.0)
        nc.scalar.dma_start(out=b_rows[0:O_TILES, :], in_=b.rearrange("(m o) -> m o", m=O_TILES))
        b_rows_f32 = const.tile([P, P], F32)
        nc.scalar.activation(out=b_rows_f32[:], in_=b_rows[:], func=IDENTITY)

        ready = quantise_chunk(transpose_chunk(0))

        b_turned = turned_pool.tile([P, BANK_WORDS], F32, tag="turned")
        nc.tensor.transpose(out=b_turned[:, 0:P], in_=b_rows_f32[:], identity=identity[:])
        bias = const.tile([P, O_TILES], F32)
        nc.scalar.activation(out=bias[:], in_=b_turned[:, 0:O_TILES], func=IDENTITY)

        acc = []
        for q in range(ALL_CHUNKS):
            m, n = divmod(q, CHUNKS)
            w_passes = ready
            if q + 1 < ALL_CHUNKS:
                banks = transpose_chunk(q + 1)
            if m == 0:
                for x_piece in range(n * CHUNK_X_PIECES, (n + 1) * CHUNK_X_PIECES):
                    prepare_x(x_piece)
            if q + 1 < ALL_CHUNKS:
                ready = quantise_chunk(banks)
            if n == 0:
                acc = []
                for j in range(GROUPS):
                    group = acc_pool.tile([P, N_MOVING], F32)
                    acc.append(group)
            multiply(n, w_passes, acc)
            if m == Z_O_TILE:
                for i in range(n * Z_TILES // CHUNKS, (n + 1) * Z_TILES // CHUNKS):
                    crop_z(i)
            if n == CHUNKS - 1:
                finish(m, acc)
